import numpy as np
import ml_dtypes

BF16 = ml_dtypes.bfloat16


def bf(x):
    return np.asarray(x, np.float32).astype(BF16)


def f32(x):
    return np.asarray(x, np.float32)


def f64(x):
    return np.asarray(x).astype(np.float64)


def striped(idx):
    return np.tile(idx.reshape(-1, 16).T, (8, 1))


C, S, N, T, M = 256, 512, 1024, 64, 128


def pos_table():
    t = np.arange(T, dtype=np.float32)[:, None]
    div = np.exp(np.arange(0, C, 2, dtype=np.float32) * np.float32(-(np.log(10000.0) / C)))
    ang = t * div
    pe = np.zeros((T, C), np.float32)
    pe[:, 0::2] = np.sin(ang)
    pe[:, 1::2] = np.cos(ang)
    return np.tile(pe.T, (1, N // T))


def setup_inputs():
    return {"x": f32(np.random.standard_normal((C, S))), "pos": f32(pos_table()), "wv": bf(np.random.standard_normal((C, C)) / np.sqrt(C)), "bv": f32(0.1 * np.random.standard_normal((C, 1))), "wc": bf(np.random.standard_normal((C, M)) / np.sqrt(C)), "bc": f32(0.1 * np.random.standard_normal((M, 1))), "offs": striped(np.random.permutation(np.tile(np.arange(S), 2))[:N])}


def reference(x, pos, wv, bv, wc, bc, offs):
    idx = offs[:16].T.reshape(-1)
    e = f64(x)[:, idx] + f64(pos)
    v = f64(wv).T @ e + f64(bv)
    return f64(wc).T @ v + f64(bc)

@@ -1,0 +1,74 @@
+import concourse.mybir as mybir
+
+F32 = mybir.dt.float32
+BF16 = mybir.dt.bfloat16
+U16 = mybir.dt.uint16
+ADD = mybir.AluOpType.add
+IDENTITY = mybir.ActivationFunctionType.Identity
+COPY = mybir.ActivationFunctionType.Copy
+
+P = 128
+C, S, N, M = 256, 512, 1024, 128
+BLOCKS = C // P
+PIECE = 512
+PIECES = N // PIECE
+OFFS_COLS = PIECE // 16
+
+FLOPS = 2 * C * C * N + 2 * C * M * N
+
+
+def tile_attentionwithpositionalencoding_kernel(tc, x, pos, wv, bv, wc, bc, offs, out):
+    nc = tc.nc
+    with (
+        tc.tile_pool(name="held", bufs=1) as held,
+        tc.tile_pool(name="work", bufs=2) as work,
+        tc.psum_pool(name="psum", bufs=2) as psum,
+    ):
+        offsets = held.tile([P, N // 16], U16, name="offsets")
+        nc.sync.dma_start(offsets[:], offs)
+
+        table = [held.tile([P, S], F32, name=f"table{b}") for b in range(BLOCKS)]
+        for b in range(BLOCKS):
+            nc.sync.dma_start(table[b][:], x[b * P : (b + 1) * P, :])
+
+        place = [[held.tile([P, PIECE], F32, name=f"place{b}_{t}") for t in range(PIECES)] for b in range(BLOCKS)]
+        for t in range(PIECES):
+            for b in range(BLOCKS):
+                nc.scalar.dma_start(place[b][t][:], pos[b * P : (b + 1) * P, t * PIECE : (t + 1) * PIECE])
+
+        wv_sb = [held.tile([P, C], BF16, name=f"wv_sb{b}") for b in range(BLOCKS)]
+        wc_sb = [held.tile([P, M], BF16, name=f"wc_sb{b}") for b in range(BLOCKS)]
+        bv_sb = [held.tile([P, 1], F32, name=f"bv_sb{b}") for b in range(BLOCKS)]
+        for b in range(BLOCKS):
+            nc.sync.dma_start(wv_sb[b][:], wv[b * P : (b + 1) * P, :])
+            nc.sync.dma_start(wc_sb[b][:], wc[b * P : (b + 1) * P, :])
+            nc.sync.dma_start(bv_sb[b][:], bv[b * P : (b + 1) * P, :])
+        bc_sb = held.tile([P, 1], F32, name="bc_sb")
+        nc.sync.dma_start(bc_sb[:], bc)
+
+        for t in range(PIECES):
+            piece_offsets = offsets[:, t * OFFS_COLS : (t + 1) * OFFS_COLS]
+
+            e_bf = []
+            for b in range(BLOCKS):
+                e_f32 = work.tile([P, PIECE], F32, name=f"e_f32_{b}")
+                nc.vector.tensor_tensor(e_f32[:], table[b][:].indirect(piece_offsets), place[b][t][:], ADD)
+                e_bf.append(work.tile([P, PIECE], BF16, name=f"e_bf{b}"))
+                nc.scalar.activation(e_bf[b][:], e_f32[:], COPY)
+
+            v_bf = []
+            for d in range(BLOCKS):
+                v_ps = psum.tile([P, PIECE], F32, name=f"v_ps{d}")
+                for b in range(BLOCKS):
+                    nc.tensor.matmul(
+                        v_ps[:], wv_sb[b][:, d * P : (d + 1) * P], e_bf[b][:], start=(b == 0), stop=(b == BLOCKS - 1)
+                    )
+                v_bf.append(work.tile([P, PIECE], BF16, name=f"v_bf{d}"))
+                nc.scalar.activation(v_bf[d][:], v_ps[:], IDENTITY, bias=bv_sb[d][:])
+
+            o_ps = psum.tile([P, PIECE], F32, name="o_ps")
+            for d in range(BLOCKS):
+                nc.tensor.matmul(o_ps[:], wc_sb[d][:], v_bf[d][:], start=(d == 0), stop=(d == BLOCKS - 1))
+            o_sb = work.tile([P, PIECE], F32, name="o_sb")
+            nc.vector.tensor_scalar_add(o_sb[:], o_ps[:], bc_sb[:])
+            nc.sync.dma_start(out[:, t * PIECE : (t + 1) * PIECE], o_sb[:])

@@ -10,7 +10,7 @@ COPY = mybir.ActivationFunctionType.Copy
 P = 128
 C, S, N, M = 256, 512, 1024, 128
 BLOCKS = C // P
-PIECE = 512
+PIECE = 256
 PIECES = N // PIECE
 OFFS_COLS = PIECE // 16
 
@@ -21,54 +21,71 @@ def tile_attentionwithpositionalencoding_kernel(tc, x, pos, wv, bv, wc, bc, offs
     nc = tc.nc
     with (
         tc.tile_pool(name="held", bufs=1) as held,
-        tc.tile_pool(name="work", bufs=2) as work,
+        tc.tile_pool(name="work", bufs=3) as work,
         tc.psum_pool(name="psum", bufs=2) as psum,
     ):
         offsets = held.tile([P, N // 16], U16, name="offsets")
-        nc.sync.dma_start(offsets[:], offs)
-
         table = [held.tile([P, S], F32, name=f"table{b}") for b in range(BLOCKS)]
-        for b in range(BLOCKS):
-            nc.sync.dma_start(table[b][:], x[b * P : (b + 1) * P, :])
-
-        place = [[held.tile([P, PIECE], F32, name=f"place{b}_{t}") for t in range(PIECES)] for b in range(BLOCKS)]
-        for t in range(PIECES):
-            for b in range(BLOCKS):
-                nc.scalar.dma_start(place[b][t][:], pos[b * P : (b + 1) * P, t * PIECE : (t + 1) * PIECE])
-
-        wv_sb = [held.tile([P, C], BF16, name=f"wv_sb{b}") for b in range(BLOCKS)]
-        wc_sb = [held.tile([P, M], BF16, name=f"wc_sb{b}") for b in range(BLOCKS)]
+        place = [held.tile([P, BLOCKS, PIECE], F32, name=f"place{t}") for t in range(PIECES)]
+        wv_sb = held.tile([P, BLOCKS, C], BF16, name="wv_sb")
+        wc_sb = held.tile([P, BLOCKS, M], BF16, name="wc_sb")
         bv_sb = [held.tile([P, 1], F32, name=f"bv_sb{b}") for b in range(BLOCKS)]
-        for b in range(BLOCKS):
-            nc.sync.dma_start(wv_sb[b][:], wv[b * P : (b + 1) * P, :])
-            nc.sync.dma_start(wc_sb[b][:], wc[b * P : (b + 1) * P, :])
-            nc.sync.dma_start(bv_sb[b][:], bv[b * P : (b + 1) * P, :])
         bc_sb = held.tile([P, 1], F32, name="bc_sb")
-        nc.sync.dma_start(bc_sb[:], bc)
 
-        for t in range(PIECES):
+        nc.sync.dma_start(offsets[:], offs)
+        nc.sync.dma_start(table[0][:], x[0:P, :])
+        nc.sync.dma_start(place[0][:], pos[:, 0:PIECE].rearrange("(b p) j -> p b j", p=P))
+        nc.sync.dma_start(table[1][:], x[P : 2 * P, :])
+        nc.sync.dma_start(wv_sb[:], wv.rearrange("(b p) d -> p b d", p=P))
+        for t in range(1, PIECES):
+            nc.sync.dma_start(place[t][:], pos[:, t * PIECE : (t + 1) * PIECE].rearrange("(b p) j -> p b j", p=P))
+        for b in range(BLOCKS):
+            nc.scalar.dma_start(bv_sb[b][:], bv[b * P : (b + 1) * P, :])
+        nc.scalar.dma_start(wc_sb[:], wc.rearrange("(b p) m -> p b m", p=P))
+        nc.scalar.dma_start(bc_sb[:], bc)
+
+        def add_bias(on_vector, dst, src, bias):
+            if on_vector:
+                nc.vector.tensor_scalar_add(dst, src, bias)
+            else:
+                nc.scalar.activation(dst, src, IDENTITY, bias=bias)
+
+        def embed_and_project(t):
             piece_offsets = offsets[:, t * OFFS_COLS : (t + 1) * OFFS_COLS]
-
             e_bf = []
             for b in range(BLOCKS):
                 e_f32 = work.tile([P, PIECE], F32, name=f"e_f32_{b}")
-                nc.vector.tensor_tensor(e_f32[:], table[b][:].indirect(piece_offsets), place[b][t][:], ADD)
+                nc.vector.tensor_tensor(e_f32[:], table[b][:].indirect(piece_offsets), place[t][:, b, :], ADD)
                 e_bf.append(work.tile([P, PIECE], BF16, name=f"e_bf{b}"))
                 nc.scalar.activation(e_bf[b][:], e_f32[:], COPY)
-
-            v_bf = []
-            for d in range(BLOCKS):
-                v_ps = psum.tile([P, PIECE], F32, name=f"v_ps{d}")
-                for b in range(BLOCKS):
+            v_ps = [psum.tile([P, PIECE], F32, name=f"v_ps{d}") for d in range(BLOCKS)]
+            for b in range(BLOCKS):
+                for d in range(BLOCKS):
                     nc.tensor.matmul(
-                        v_ps[:], wv_sb[b][:, d * P : (d + 1) * P], e_bf[b][:], start=(b == 0), stop=(b == BLOCKS - 1)
+                        v_ps[d][:], wv_sb[:, b, d * P : (d + 1) * P], e_bf[b][:], start=(b == 0), stop=(b == BLOCKS - 1)
                     )
-                v_bf.append(work.tile([P, PIECE], BF16, name=f"v_bf{d}"))
-                nc.scalar.activation(v_bf[d][:], v_ps[:], IDENTITY, bias=bv_sb[d][:])
+            return v_ps
 
+        def bias_and_classify(v_ps, vector_is_free):
             o_ps = psum.tile([P, PIECE], F32, name="o_ps")
             for d in range(BLOCKS):
-                nc.tensor.matmul(o_ps[:], wc_sb[d][:], v_bf[d][:], start=(d == 0), stop=(d == BLOCKS - 1))
+                v_bf = work.tile([P, PIECE], BF16, name=f"v_bf{d}")
+                add_bias(vector_is_free and d == 1, v_bf[:], v_ps[d][:], bv_sb[d][:])
+                nc.tensor.matmul(o_ps[:], wc_sb[:, d, :], v_bf[:], start=(d == 0), stop=(d == BLOCKS - 1))
+            return o_ps
+
+        def bias_and_store(t, o_ps, vector_is_free):
             o_sb = work.tile([P, PIECE], F32, name="o_sb")
-            nc.vector.tensor_scalar_add(o_sb[:], o_ps[:], bc_sb[:])
+            add_bias(vector_is_free, o_sb[:], o_ps[:], bc_sb[:])
             nc.sync.dma_start(out[:, t * PIECE : (t + 1) * PIECE], o_sb[:])
+
+        v_sums = {}
+        o_sums = {}
+        for i in range(PIECES + 2):
+            vector_is_free = i >= PIECES
+            if i < PIECES:
+                v_sums[i] = embed_and_project(i)
+            if 0 <= i - 1 < PIECES:
+                o_sums[i - 1] = bias_and_classify(v_sums[i - 1], vector_is_free)
+            if 0 <= i - 2:
+                bias_and_store(i - 2, o_sums[i - 2], vector_is_free)

@@ -14,6 +14,9 @@ PIECE = 256
 PIECES = N // PIECE
 OFFS_COLS = PIECE // 16
 
+WARM_COLS = 512
+WARM_MATMULS = 8
+
 FLOPS = 2 * C * C * N + 2 * C * M * N
 
 
@@ -23,6 +26,7 @@ def tile_attentionwithpositionalencoding_kernel(tc, x, pos, wv, bv, wc, bc, offs
         tc.tile_pool(name="held", bufs=1) as held,
         tc.tile_pool(name="work", bufs=3) as work,
         tc.psum_pool(name="psum", bufs=2) as psum,
+        tc.psum_pool(name="spare", bufs=1) as spare,
     ):
         offsets = held.tile([P, N // 16], U16, name="offsets")
         table = [held.tile([P, S], F32, name=f"table{b}") for b in range(BLOCKS)]
@@ -43,6 +47,12 @@ def tile_attentionwithpositionalencoding_kernel(tc, x, pos, wv, bv, wc, bc, offs
             nc.scalar.dma_start(bv_sb[b][:], bv[b * P : (b + 1) * P, :])
         nc.scalar.dma_start(wc_sb[:], wc.rearrange("(b p) m -> p b m", p=P))
         nc.scalar.dma_start(bc_sb[:], bc)
+
+        zeros = held.tile([P, WARM_COLS], BF16, name="zeros")
+        nc.vector.memset(zeros[:], 0.0)
+        unused = spare.tile([P, WARM_COLS], F32, name="unused")
+        for k in range(WARM_MATMULS):
+            nc.tensor.matmul(unused[:], zeros[:, 0:P], zeros[:], start=True, stop=True)
 
         def add_bias(on_vector, dst, src, bias):
             if on_vector:

@@ -14,9 +14,6 @@ PIECE = 256
 PIECES = N // PIECE
 OFFS_COLS = PIECE // 16
 
-WARM_COLS = 512
-WARM_MATMULS = 8
-
 FLOPS = 2 * C * C * N + 2 * C * M * N
 
 
@@ -25,8 +22,8 @@ def tile_attentionwithpositionalencoding_kernel(tc, x, pos, wv, bv, wc, bc, offs
     with (
         tc.tile_pool(name="held", bufs=1) as held,
         tc.tile_pool(name="work", bufs=3) as work,
-        tc.psum_pool(name="psum", bufs=2) as psum,
-        tc.psum_pool(name="spare", bufs=1) as spare,
+        tc.psum_pool(name="v_banks", bufs=2) as v_banks,
+        tc.psum_pool(name="o_banks", bufs=PIECES) as o_banks,
     ):
         offsets = held.tile([P, N // 16], U16, name="offsets")
         table = [held.tile([P, S], F32, name=f"table{b}") for b in range(BLOCKS)]
@@ -48,18 +45,6 @@ def tile_attentionwithpositionalencoding_kernel(tc, x, pos, wv, bv, wc, bc, offs
         nc.scalar.dma_start(wc_sb[:], wc.rearrange("(b p) m -> p b m", p=P))
         nc.scalar.dma_start(bc_sb[:], bc)
 
-        zeros = held.tile([P, WARM_COLS], BF16, name="zeros")
-        nc.vector.memset(zeros[:], 0.0)
-        unused = spare.tile([P, WARM_COLS], F32, name="unused")
-        for k in range(WARM_MATMULS):
-            nc.tensor.matmul(unused[:], zeros[:, 0:P], zeros[:], start=True, stop=True)
-
-        def add_bias(on_vector, dst, src, bias):
-            if on_vector:
-                nc.vector.tensor_scalar_add(dst, src, bias)
-            else:
-                nc.scalar.activation(dst, src, IDENTITY, bias=bias)
-
         def embed_and_project(t):
             piece_offsets = offsets[:, t * OFFS_COLS : (t + 1) * OFFS_COLS]
             e_bf = []
@@ -68,7 +53,7 @@ def tile_attentionwithpositionalencoding_kernel(tc, x, pos, wv, bv, wc, bc, offs
                 nc.vector.tensor_tensor(e_f32[:], table[b][:].indirect(piece_offsets), place[t][:, b, :], ADD)
                 e_bf.append(work.tile([P, PIECE], BF16, name=f"e_bf{b}"))
                 nc.scalar.activation(e_bf[b][:], e_f32[:], COPY)
-            v_ps = [psum.tile([P, PIECE], F32, name=f"v_ps{d}") for d in range(BLOCKS)]
+            v_ps = [v_banks.tile([P, PIECE], F32, name=f"v_ps{d}") for d in range(BLOCKS)]
             for b in range(BLOCKS):
                 for d in range(BLOCKS):
                     nc.tensor.matmul(
@@ -76,26 +61,22 @@ def tile_attentionwithpositionalencoding_kernel(tc, x, pos, wv, bv, wc, bc, offs
                     )
             return v_ps
 
-        def bias_and_classify(v_ps, vector_is_free):
-            o_ps = psum.tile([P, PIECE], F32, name="o_ps")
+        def bias_and_classify(v_ps):
+            o_ps = o_banks.tile([P, PIECE], F32, name="o_ps")
             for d in range(BLOCKS):
                 v_bf = work.tile([P, PIECE], BF16, name=f"v_bf{d}")
-                add_bias(vector_is_free and d == 1, v_bf[:], v_ps[d][:], bv_sb[d][:])
+                nc.scalar.activation(v_bf[:], v_ps[d][:], IDENTITY, bias=bv_sb[d][:])
                 nc.tensor.matmul(o_ps[:], wc_sb[:, d, :], v_bf[:], start=(d == 0), stop=(d == BLOCKS - 1))
             return o_ps
 
-        def bias_and_store(t, o_ps, vector_is_free):
-            o_sb = work.tile([P, PIECE], F32, name="o_sb")
-            add_bias(vector_is_free, o_sb[:], o_ps[:], bc_sb[:])
-            nc.sync.dma_start(out[:, t * PIECE : (t + 1) * PIECE], o_sb[:])
+        v_sums = [embed_and_project(0)]
+        o_sums = []
+        for t in range(1, PIECES):
+            v_sums.append(embed_and_project(t))
+            o_sums.append(bias_and_classify(v_sums[t - 1]))
+        o_sums.append(bias_and_classify(v_sums[PIECES - 1]))
 
-        v_sums = {}
-        o_sums = {}
-        for i in range(PIECES + 2):
-            vector_is_free = i >= PIECES
-            if i < PIECES:
-                v_sums[i] = embed_and_project(i)
-            if 0 <= i - 1 < PIECES:
-                o_sums[i - 1] = bias_and_classify(v_sums[i - 1], vector_is_free)
-            if 0 <= i - 2:
-                bias_and_store(i - 2, o_sums[i - 2], vector_is_free)
+        for t in range(PIECES):
+            o_sb = work.tile([P, PIECE], F32, name="o_sb")
+            nc.vector.tensor_scalar_add(o_sb[:], o_sums[t][:], bc_sb[:])
+            nc.sync.dma_start(out[:, t * PIECE : (t + 1) * PIECE], o_sb[:])

@@ -61,11 +61,14 @@ def tile_attentionwithpositionalencoding_kernel(tc, x, pos, wv, bv, wc, bc, offs
                     )
             return v_ps
 
-        def bias_and_classify(v_ps):
+        def bias_and_classify(v_ps, vector_helps):
             o_ps = o_banks.tile([P, PIECE], F32, name="o_ps")
             for d in range(BLOCKS):
                 v_bf = work.tile([P, PIECE], BF16, name=f"v_bf{d}")
-                nc.scalar.activation(v_bf[:], v_ps[d][:], IDENTITY, bias=bv_sb[d][:])
+                if vector_helps and d == 1:
+                    nc.vector.tensor_scalar_add(v_bf[:], v_ps[d][:], bv_sb[d][:])
+                else:
+                    nc.scalar.activation(v_bf[:], v_ps[d][:], IDENTITY, bias=bv_sb[d][:])
                 nc.tensor.matmul(o_ps[:], wc_sb[:, d, :], v_bf[:], start=(d == 0), stop=(d == BLOCKS - 1))
             return o_ps
 
@@ -73,10 +76,15 @@ def tile_attentionwithpositionalencoding_kernel(tc, x, pos, wv, bv, wc, bc, offs
         o_sums = []
         for t in range(1, PIECES):
             v_sums.append(embed_and_project(t))
-            o_sums.append(bias_and_classify(v_sums[t - 1]))
-        o_sums.append(bias_and_classify(v_sums[PIECES - 1]))
+            o_sums.append(bias_and_classify(v_sums[t - 1], False))
 
-        for t in range(PIECES):
+        def bias_and_store(t):
             o_sb = work.tile([P, PIECE], F32, name="o_sb")
             nc.vector.tensor_scalar_add(o_sb[:], o_sums[t][:], bc_sb[:])
             nc.sync.dma_start(out[:, t * PIECE : (t + 1) * PIECE], o_sb[:])
+
+        for t in range(PIECES - 2):
+            bias_and_store(t)
+        o_sums.append(bias_and_classify(v_sums[PIECES - 1], True))
+        for t in range(PIECES - 2, PIECES):
+            bias_and_store(t)

@@ -45,14 +45,17 @@ def tile_attentionwithpositionalencoding_kernel(tc, x, pos, wv, bv, wc, bc, offs
         nc.scalar.dma_start(wc_sb[:], wc.rearrange("(b p) m -> p b m", p=P))
         nc.scalar.dma_start(bc_sb[:], bc)
 
-        def embed_and_project(t):
+        def embed_and_project(t, vector_helps):
             piece_offsets = offsets[:, t * OFFS_COLS : (t + 1) * OFFS_COLS]
             e_bf = []
             for b in range(BLOCKS):
                 e_f32 = work.tile([P, PIECE], F32, name=f"e_f32_{b}")
                 nc.vector.tensor_tensor(e_f32[:], table[b][:].indirect(piece_offsets), place[t][:, b, :], ADD)
                 e_bf.append(work.tile([P, PIECE], BF16, name=f"e_bf{b}"))
-                nc.scalar.activation(e_bf[b][:], e_f32[:], COPY)
+                if vector_helps and b == 1:
+                    nc.vector.tensor_copy(e_bf[b][:], e_f32[:])
+                else:
+                    nc.scalar.activation(e_bf[b][:], e_f32[:], COPY)
             v_ps = [v_banks.tile([P, PIECE], F32, name=f"v_ps{d}") for d in range(BLOCKS)]
             for b in range(BLOCKS):
                 for d in range(BLOCKS):
@@ -72,10 +75,10 @@ def tile_attentionwithpositionalencoding_kernel(tc, x, pos, wv, bv, wc, bc, offs
                 nc.tensor.matmul(o_ps[:], wc_sb[:, d, :], v_bf[:], start=(d == 0), stop=(d == BLOCKS - 1))
             return o_ps
 
-        v_sums = [embed_and_project(0)]
+        v_sums = [embed_and_project(0, False)]
         o_sums = []
         for t in range(1, PIECES):
-            v_sums.append(embed_and_project(t))
+            v_sums.append(embed_and_project(t, t == PIECES - 1))
             o_sums.append(bias_and_classify(v_sums[t - 1], False))
 
         def bias_and_store(t):

@@ -13,6 +13,7 @@ BLOCKS = C // P
 PIECE = 256
 PIECES = N // PIECE
 OFFS_COLS = PIECE // 16
+LAST = PIECES - 1
 
 FLOPS = 2 * C * C * N + 2 * C * M * N
 
@@ -27,67 +28,82 @@ def tile_attentionwithpositionalencoding_kernel(tc, x, pos, wv, bv, wc, bc, offs
     ):
         offsets = held.tile([P, N // 16], U16, name="offsets")
         table = [held.tile([P, S], F32, name=f"table{b}") for b in range(BLOCKS)]
-        place = [held.tile([P, BLOCKS, PIECE], F32, name=f"place{t}") for t in range(PIECES)]
+        place = held.tile([P, BLOCKS, N], F32, name="place")
         wv_sb = held.tile([P, BLOCKS, C], BF16, name="wv_sb")
         wc_sb = held.tile([P, BLOCKS, M], BF16, name="wc_sb")
-        bv_sb = [held.tile([P, 1], F32, name=f"bv_sb{b}") for b in range(BLOCKS)]
+        bv_sb = held.tile([P, BLOCKS], F32, name="bv_sb")
         bc_sb = held.tile([P, 1], F32, name="bc_sb")
+
+        def tokens(first, after):
+            return slice(first * PIECE, after * PIECE)
+
+        def load_place_block(b, first, after):
+            nc.sync.dma_start(place[:, b, tokens(first, after)], pos[b * P : (b + 1) * P, tokens(first, after)])
+
+        def load_place_piece(t):
+            nc.sync.dma_start(
+                place[:, :, tokens(t, t + 1)], pos[:, tokens(t, t + 1)].rearrange("(b p) j -> p b j", p=P)
+            )
 
         nc.sync.dma_start(offsets[:], offs)
         nc.sync.dma_start(table[0][:], x[0:P, :])
-        nc.sync.dma_start(place[0][:], pos[:, 0:PIECE].rearrange("(b p) j -> p b j", p=P))
+        load_place_block(0, 0, 1)
+        load_place_block(0, 1, 2)
         nc.sync.dma_start(table[1][:], x[P : 2 * P, :])
+        load_place_block(1, 0, 2)
         nc.sync.dma_start(wv_sb[:], wv.rearrange("(b p) d -> p b d", p=P))
-        for t in range(1, PIECES):
-            nc.sync.dma_start(place[t][:], pos[:, t * PIECE : (t + 1) * PIECE].rearrange("(b p) j -> p b j", p=P))
-        for b in range(BLOCKS):
-            nc.scalar.dma_start(bv_sb[b][:], bv[b * P : (b + 1) * P, :])
+        for t in range(2, PIECES):
+            load_place_piece(t)
+        nc.scalar.dma_start(bv_sb[:], bv.rearrange("(b p) o -> p (b o)", p=P))
         nc.scalar.dma_start(wc_sb[:], wc.rearrange("(b p) m -> p b m", p=P))
         nc.scalar.dma_start(bc_sb[:], bc)
 
-        def embed_and_project(t, vector_helps):
-            piece_offsets = offsets[:, t * OFFS_COLS : (t + 1) * OFFS_COLS]
-            e_bf = []
-            for b in range(BLOCKS):
-                e_f32 = work.tile([P, PIECE], F32, name=f"e_f32_{b}")
-                nc.vector.tensor_tensor(e_f32[:], table[b][:].indirect(piece_offsets), place[t][:, b, :], ADD)
-                e_bf.append(work.tile([P, PIECE], BF16, name=f"e_bf{b}"))
-                if vector_helps and b == 1:
-                    nc.vector.tensor_copy(e_bf[b][:], e_f32[:])
-                else:
-                    nc.scalar.activation(e_bf[b][:], e_f32[:], COPY)
-            v_ps = [v_banks.tile([P, PIECE], F32, name=f"v_ps{d}") for d in range(BLOCKS)]
-            for b in range(BLOCKS):
-                for d in range(BLOCKS):
-                    nc.tensor.matmul(
-                        v_ps[d][:], wv_sb[:, b, d * P : (d + 1) * P], e_bf[b][:], start=(b == 0), stop=(b == BLOCKS - 1)
-                    )
-            return v_ps
+        v_sums = {}
+        o_sums = {}
 
-        def bias_and_classify(v_ps, vector_helps):
-            o_ps = o_banks.tile([P, PIECE], F32, name="o_ps")
+        def embed_and_project(b, t):
+            e_f32 = work.tile([P, PIECE], F32, name=f"e_f32_{b}")
+            piece_offsets = offsets[:, t * OFFS_COLS : (t + 1) * OFFS_COLS]
+            nc.vector.tensor_tensor(e_f32[:], table[b][:].indirect(piece_offsets), place[:, b, tokens(t, t + 1)], ADD)
+            e_bf = work.tile([P, PIECE], BF16, name=f"e_bf{b}")
+            if t == LAST and b == BLOCKS - 1:
+                nc.vector.tensor_copy(e_bf[:], e_f32[:])
+            else:
+                nc.scalar.activation(e_bf[:], e_f32[:], COPY)
+            if b == 0:
+                v_sums[t] = [v_banks.tile([P, PIECE], F32, name=f"v_ps{d}") for d in range(BLOCKS)]
+            for d in range(BLOCKS):
+                nc.tensor.matmul(
+                    v_sums[t][d][:], wv_sb[:, b, d * P : (d + 1) * P], e_bf[:], start=(b == 0), stop=(b == BLOCKS - 1)
+                )
+
+        def bias_and_classify(t):
+            o_sums[t] = o_banks.tile([P, PIECE], F32, name="o_ps")
             for d in range(BLOCKS):
                 v_bf = work.tile([P, PIECE], BF16, name=f"v_bf{d}")
-                if vector_helps and d == 1:
-                    nc.vector.tensor_scalar_add(v_bf[:], v_ps[d][:], bv_sb[d][:])
+                if t == LAST and d == BLOCKS - 1:
+                    nc.vector.tensor_scalar_add(v_bf[:], v_sums[t][d][:], bv_sb[:, d : d + 1])
                 else:
-                    nc.scalar.activation(v_bf[:], v_ps[d][:], IDENTITY, bias=bv_sb[d][:])
-                nc.tensor.matmul(o_ps[:], wc_sb[:, d, :], v_bf[:], start=(d == 0), stop=(d == BLOCKS - 1))
-            return o_ps
-
-        v_sums = [embed_and_project(0, False)]
-        o_sums = []
-        for t in range(1, PIECES):
-            v_sums.append(embed_and_project(t, t == PIECES - 1))
-            o_sums.append(bias_and_classify(v_sums[t - 1], False))
+                    nc.scalar.activation(v_bf[:], v_sums[t][d][:], IDENTITY, bias=bv_sb[:, d : d + 1])
+                nc.tensor.matmul(o_sums[t][:], wc_sb[:, d, :], v_bf[:], start=(d == 0), stop=(d == BLOCKS - 1))
 
         def bias_and_store(t):
-            o_sb = work.tile([P, PIECE], F32, name="o_sb")
+            o_sb = held.tile([P, PIECE], F32, name=f"o_sb{t}")
             nc.vector.tensor_scalar_add(o_sb[:], o_sums[t][:], bc_sb[:])
-            nc.sync.dma_start(out[:, t * PIECE : (t + 1) * PIECE], o_sb[:])
+            nc.sync.dma_start(out[:, tokens(t, t + 1)], o_sb[:])
+
+        embed_and_project(0, 0)
+        embed_and_project(0, 1)
+        embed_and_project(1, 0)
+        embed_and_project(1, 1)
+        bias_and_classify(0)
+        for t in range(2, PIECES):
+            for b in range(BLOCKS):
+                embed_and_project(b, t)
+            bias_and_classify(t - 1)
 
         for t in range(PIECES - 2):
             bias_and_store(t)
-        o_sums.append(bias_and_classify(v_sums[PIECES - 1], True))
+        bias_and_classify(LAST)
         for t in range(PIECES - 2, PIECES):
             bias_and_store(t)

@@ -40,9 +40,9 @@ def tile_attentionwithpositionalencoding_kernel(tc, x, pos, wv, bv, wc, bc, offs
         def load_place_block(b, first, after):
             nc.sync.dma_start(place[:, b, tokens(first, after)], pos[b * P : (b + 1) * P, tokens(first, after)])
 
-        def load_place_piece(t):
+        def load_place_pieces(first, after):
             nc.sync.dma_start(
-                place[:, :, tokens(t, t + 1)], pos[:, tokens(t, t + 1)].rearrange("(b p) j -> p b j", p=P)
+                place[:, :, tokens(first, after)], pos[:, tokens(first, after)].rearrange("(b p) j -> p b j", p=P)
             )
 
         nc.sync.dma_start(offsets[:], offs)
@@ -52,11 +52,10 @@ def tile_attentionwithpositionalencoding_kernel(tc, x, pos, wv, bv, wc, bc, offs
         nc.sync.dma_start(table[1][:], x[P : 2 * P, :])
         load_place_block(1, 0, 2)
         nc.sync.dma_start(wv_sb[:], wv.rearrange("(b p) d -> p b d", p=P))
-        for t in range(2, PIECES):
-            load_place_piece(t)
-        nc.scalar.dma_start(bv_sb[:], bv.rearrange("(b p) o -> p (b o)", p=P))
-        nc.scalar.dma_start(wc_sb[:], wc.rearrange("(b p) m -> p b m", p=P))
-        nc.scalar.dma_start(bc_sb[:], bc)
+        load_place_pieces(2, PIECES)
+        nc.sync.dma_start(bv_sb[:], bv.rearrange("(b p) o -> p (b o)", p=P))
+        nc.sync.dma_start(wc_sb[:], wc.rearrange("(b p) m -> p b m", p=P))
+        nc.sync.dma_start(bc_sb[:], bc)
 
         v_sums = {}
         o_sums = {}

@@ -10,9 +10,9 @@ COPY = mybir.ActivationFunctionType.Copy
 P = 128
 C, S, N, M = 256, 512, 1024, 128
 BLOCKS = C // P
-PIECE = 256
-PIECES = N // PIECE
-OFFS_COLS = PIECE // 16
+WIDTHS = (256, 384, 256, 128)
+STARTS = tuple(sum(WIDTHS[:t]) for t in range(len(WIDTHS)))
+PIECES = len(WIDTHS)
 LAST = PIECES - 1
 
 FLOPS = 2 * C * C * N + 2 * C * M * N
@@ -24,7 +24,7 @@ def tile_attentionwithpositionalencoding_kernel(tc, x, pos, wv, bv, wc, bc, offs
         tc.tile_pool(name="held", bufs=1) as held,
         tc.tile_pool(name="work", bufs=3) as work,
         tc.psum_pool(name="v_banks", bufs=2) as v_banks,
-        tc.psum_pool(name="o_banks", bufs=PIECES) as o_banks,
+        tc.psum_pool(name="o_banks", bufs=4) as o_banks,
     ):
         offsets = held.tile([P, N // 16], U16, name="offsets")
         table = [held.tile([P, S], F32, name=f"table{b}") for b in range(BLOCKS)]
@@ -34,25 +34,23 @@ def tile_attentionwithpositionalencoding_kernel(tc, x, pos, wv, bv, wc, bc, offs
         bv_sb = held.tile([P, BLOCKS], F32, name="bv_sb")
         bc_sb = held.tile([P, 1], F32, name="bc_sb")
 
-        def tokens(first, after):
-            return slice(first * PIECE, after * PIECE)
+        def tokens(t):
+            return slice(STARTS[t], STARTS[t] + WIDTHS[t])
 
-        def load_place_block(b, first, after):
-            nc.sync.dma_start(place[:, b, tokens(first, after)], pos[b * P : (b + 1) * P, tokens(first, after)])
+        def load_place_block(b, cols):
+            nc.sync.dma_start(place[:, b, cols], pos[b * P : (b + 1) * P, cols])
 
-        def load_place_pieces(first, after):
-            nc.sync.dma_start(
-                place[:, :, tokens(first, after)], pos[:, tokens(first, after)].rearrange("(b p) j -> p b j", p=P)
-            )
+        def load_place(cols):
+            nc.sync.dma_start(place[:, :, cols], pos[:, cols].rearrange("(b p) j -> p b j", p=P))
 
         nc.sync.dma_start(offsets[:], offs)
         nc.sync.dma_start(table[0][:], x[0:P, :])
-        load_place_block(0, 0, 1)
-        load_place_block(0, 1, 2)
+        load_place_block(0, tokens(0))
+        load_place_block(0, tokens(1))
         nc.sync.dma_start(table[1][:], x[P : 2 * P, :])
-        load_place_block(1, 0, 2)
+        load_place_block(1, slice(0, STARTS[2]))
         nc.sync.dma_start(wv_sb[:], wv.rearrange("(b p) d -> p b d", p=P))
-        load_place_pieces(2, PIECES)
+        load_place(slice(STARTS[2], N))
         nc.sync.dma_start(bv_sb[:], bv.rearrange("(b p) o -> p (b o)", p=P))
         nc.sync.dma_start(wc_sb[:], wc.rearrange("(b p) m -> p b m", p=P))
         nc.sync.dma_start(bc_sb[:], bc)
@@ -61,25 +59,25 @@ def tile_attentionwithpositionalencoding_kernel(tc, x, pos, wv, bv, wc, bc, offs
         o_sums = {}
 
         def embed_and_project(b, t):
-            e_f32 = work.tile([P, PIECE], F32, name=f"e_f32_{b}")
-            piece_offsets = offsets[:, t * OFFS_COLS : (t + 1) * OFFS_COLS]
-            nc.vector.tensor_tensor(e_f32[:], table[b][:].indirect(piece_offsets), place[:, b, tokens(t, t + 1)], ADD)
-            e_bf = work.tile([P, PIECE], BF16, name=f"e_bf{b}")
+            e_f32 = work.tile([P, WIDTHS[t]], F32, name=f"e_f32_{b}")
+            piece_offsets = offsets[:, STARTS[t] // 16 : (STARTS[t] + WIDTHS[t]) // 16]
+            nc.vector.tensor_tensor(e_f32[:], table[b][:].indirect(piece_offsets), place[:, b, tokens(t)], ADD)
+            e_bf = work.tile([P, WIDTHS[t]], BF16, name=f"e_bf{b}")
             if t == LAST and b == BLOCKS - 1:
                 nc.vector.tensor_copy(e_bf[:], e_f32[:])
             else:
                 nc.scalar.activation(e_bf[:], e_f32[:], COPY)
             if b == 0:
-                v_sums[t] = [v_banks.tile([P, PIECE], F32, name=f"v_ps{d}") for d in range(BLOCKS)]
+                v_sums[t] = [v_banks.tile([P, WIDTHS[t]], F32, name=f"v_ps{d}") for d in range(BLOCKS)]
             for d in range(BLOCKS):
                 nc.tensor.matmul(
                     v_sums[t][d][:], wv_sb[:, b, d * P : (d + 1) * P], e_bf[:], start=(b == 0), stop=(b == BLOCKS - 1)
                 )
 
         def bias_and_classify(t):
-            o_sums[t] = o_banks.tile([P, PIECE], F32, name="o_ps")
+            o_sums[t] = o_banks.tile([P, WIDTHS[t]], F32, name="o_ps")
             for d in range(BLOCKS):
-                v_bf = work.tile([P, PIECE], BF16, name=f"v_bf{d}")
+                v_bf = work.tile([P, WIDTHS[t]], BF16, name=f"v_bf{d}")
                 if t == LAST and d == BLOCKS - 1:
                     nc.vector.tensor_scalar_add(v_bf[:], v_sums[t][d][:], bv_sb[:, d : d + 1])
                 else:
@@ -87,9 +85,9 @@ def tile_attentionwithpositionalencoding_kernel(tc, x, pos, wv, bv, wc, bc, offs
                 nc.tensor.matmul(o_sums[t][:], wc_sb[:, d, :], v_bf[:], start=(d == 0), stop=(d == BLOCKS - 1))
 
         def bias_and_store(t):
-            o_sb = held.tile([P, PIECE], F32, name=f"o_sb{t}")
+            o_sb = held.tile([P, WIDTHS[t]], F32, name=f"o_sb{t}")
             nc.vector.tensor_scalar_add(o_sb[:], o_sums[t][:], bc_sb[:])
-            nc.sync.dma_start(out[:, tokens(t, t + 1)], o_sb[:])
+            nc.sync.dma_start(out[:, tokens(t)], o_sb[:])
 
         embed_and_project(0, 0)
         embed_and_project(0, 1)
@@ -101,8 +99,8 @@ def tile_attentionwithpositionalencoding_kernel(tc, x, pos, wv, bv, wc, bc, offs
                 embed_and_project(b, t)
             bias_and_classify(t - 1)
 
-        for t in range(PIECES - 2):
+        for t in range(2):
             bias_and_store(t)
         bias_and_classify(LAST)
-        for t in range(PIECES - 2, PIECES):
+        for t in range(2, PIECES):
             bias_and_store(t)

@@ -48,8 +48,9 @@ def tile_attentionwithpositionalencoding_kernel(tc, x, pos, wv, bv, wc, bc, offs
         load_place_block(0, tokens(0))
         load_place_block(0, tokens(1))
         nc.sync.dma_start(table[1][:], x[P : 2 * P, :])
-        load_place_block(1, slice(0, STARTS[2]))
+        load_place_block(1, tokens(0))
         nc.sync.dma_start(wv_sb[:], wv.rearrange("(b p) d -> p b d", p=P))
+        load_place_block(1, tokens(1))
         load_place(slice(STARTS[2], N))
         nc.sync.dma_start(bv_sb[:], bv.rearrange("(b p) o -> p (b o)", p=P))
         nc.sync.dma_start(wc_sb[:], wc.rearrange("(b p) m -> p b m", p=P))

import concourse.mybir as mybir

F32 = mybir.dt.float32
BF16 = mybir.dt.bfloat16
U16 = mybir.dt.uint16
ADD = mybir.AluOpType.add
IDENTITY = mybir.ActivationFunctionType.Identity
COPY = mybir.ActivationFunctionType.Copy

P = 128
C, S, N, M = 256, 512, 1024, 128
BLOCKS = C // P
WIDTHS = (256, 384, 256, 128)
STARTS = tuple(sum(WIDTHS[:t]) for t in range(len(WIDTHS)))
PIECES = len(WIDTHS)
LAST = PIECES - 1

FLOPS = 2 * C * C * N + 2 * C * M * N


def tile_attentionwithpositionalencoding_kernel(tc, x, pos, wv, bv, wc, bc, offs, out):
    nc = tc.nc
    with (
        tc.tile_pool(name="held", bufs=1) as held,
        tc.tile_pool(name="work", bufs=3) as work,
        tc.psum_pool(name="v_banks", bufs=2) as v_banks,
        tc.psum_pool(name="o_banks", bufs=4) as o_banks,
    ):
        offsets = held.tile([P, N // 16], U16, name="offsets")
        table = [held.tile([P, S], F32, name=f"table{b}") for b in range(BLOCKS)]
        place = held.tile([P, BLOCKS, N], F32, name="place")
        wv_sb = held.tile([P, BLOCKS, C], BF16, name="wv_sb")
        wc_sb = held.tile([P, BLOCKS, M], BF16, name="wc_sb")
        bv_sb = held.tile([P, BLOCKS], F32, name="bv_sb")
        bc_sb = held.tile([P, 1], F32, name="bc_sb")

        def tokens(t):
            return slice(STARTS[t], STARTS[t] + WIDTHS[t])

        def load_place_block(b, cols):
            nc.sync.dma_start(place[:, b, cols], pos[b * P : (b + 1) * P, cols])

        def load_place(cols):
            nc.sync.dma_start(place[:, :, cols], pos[:, cols].rearrange("(b p) j -> p b j", p=P))

        nc.sync.dma_start(offsets[:], offs)
        nc.sync.dma_start(table[0][:], x[0:P, :])
        load_place_block(0, tokens(0))
        load_place_block(0, tokens(1))
        nc.sync.dma_start(table[1][:], x[P : 2 * P, :])
        load_place_block(1, tokens(0))
        nc.sync.dma_start(wv_sb[:], wv.rearrange("(b p) d -> p b d", p=P))
        load_place_block(1, tokens(1))
        load_place(slice(STARTS[2], N))
        nc.sync.dma_start(bv_sb[:], bv.rearrange("(b p) o -> p (b o)", p=P))
        nc.sync.dma_start(wc_sb[:], wc.rearrange("(b p) m -> p b m", p=P))
        nc.sync.dma_start(bc_sb[:], bc)

        v_sums = {}
        o_sums = {}

        def embed_and_project(b, t):
            e_f32 = work.tile([P, WIDTHS[t]], F32, name=f"e_f32_{b}")
            piece_offsets = offsets[:, STARTS[t] // 16 : (STARTS[t] + WIDTHS[t]) // 16]
            nc.vector.tensor_tensor(e_f32[:], table[b][:].indirect(piece_offsets), place[:, b, tokens(t)], ADD)
            e_bf = work.tile([P, WIDTHS[t]], BF16, name=f"e_bf{b}")
            if t == LAST and b == BLOCKS - 1:
                nc.vector.tensor_copy(e_bf[:], e_f32[:])
            else:
                nc.scalar.activation(e_bf[:], e_f32[:], COPY)
            if b == 0:
                v_sums[t] = [v_banks.tile([P, WIDTHS[t]], F32, name=f"v_ps{d}") for d in range(BLOCKS)]
            for d in range(BLOCKS):
                nc.tensor.matmul(
                    v_sums[t][d][:], wv_sb[:, b, d * P : (d + 1) * P], e_bf[:], start=(b == 0), stop=(b == BLOCKS - 1)
                )

        def bias_and_classify(t):
            o_sums[t] = o_banks.tile([P, WIDTHS[t]], F32, name="o_ps")
            for d in range(BLOCKS):
                v_bf = work.tile([P, WIDTHS[t]], BF16, name=f"v_bf{d}")
                if t == LAST and d == BLOCKS - 1:
                    nc.vector.tensor_scalar_add(v_bf[:], v_sums[t][d][:], bv_sb[:, d : d + 1])
                else:
                    nc.scalar.activation(v_bf[:], v_sums[t][d][:], IDENTITY, bias=bv_sb[:, d : d + 1])
                nc.tensor.matmul(o_sums[t][:], wc_sb[:, d, :], v_bf[:], start=(d == 0), stop=(d == BLOCKS - 1))

        def bias_and_store(t):
            o_sb = held.tile([P, WIDTHS[t]], F32, name=f"o_sb{t}")
            nc.vector.tensor_scalar_add(o_sb[:], o_sums[t][:], bc_sb[:])
            nc.sync.dma_start(out[:, tokens(t)], o_sb[:])

        embed_and_project(0, 0)
        embed_and_project(0, 1)
        embed_and_project(1, 0)
        embed_and_project(1, 1)
        bias_and_classify(0)
        for t in range(2, PIECES):
            for b in range(BLOCKS):
                embed_and_project(b, t)
            bias_and_classify(t - 1)

        for t in range(2):
            bias_and_store(t)
        bias_and_classify(LAST)
        for t in range(2, PIECES):
            bias_and_store(t)
